import numpy as np
import ml_dtypes


def mxq(x, axis, fmt="e4m3"):
    dtype, down = {"e4m3": (ml_dtypes.float8_e4m3fn, 7), "e5m2": (ml_dtypes.float8_e5m2, 14)}[fmt]
    v = np.moveaxis(np.asarray(x, np.float32).astype(ml_dtypes.bfloat16).astype(np.float64), axis, -1)
    blocks = v.reshape(v.shape[:-1] + (-1, 32))
    amax = np.abs(blocks).max(-1, keepdims=True)
    byte = np.maximum(np.where(amax > 0, np.frexp(amax)[1] - 1 + 127, 0) - down, 1)
    scale = np.exp2(byte - 127.0)
    codes = (blocks / scale).astype(np.float32).astype(dtype).astype(np.float64)
    return np.moveaxis((codes * scale).reshape(v.shape), -1, axis)


WIDE = False


def mx_kscale(k):
    if not WIDE:
        return np.ones(k)
    levels = np.array([10, -10, 5, -5, 0])
    a = np.random.permutation(np.resize(levels, k // 512 * 4)).reshape(k // 512, 4)
    idx = np.arange(k)
    return np.exp2(a[idx // 512, idx % 128 // 32])


BF16 = ml_dtypes.bfloat16


def bf(x):
    return np.asarray(x, np.float32).astype(BF16)


def f64(x):
    return np.asarray(x).astype(np.float64)


C, N, G = 1024, 1024, 128


def setup_inputs():
    s = mx_kscale(C)
    cen = np.random.standard_normal((C, G)) * 2.5 / np.sqrt(C)
    grp = np.random.randint(0, G, N)
    return {"vma": bf(cen[:, grp] + np.random.standard_normal((C, N)) * 1.2 / np.sqrt(C)),
            "vmr": bf(np.maximum(np.random.standard_normal((C, N)), 0.0) * s[:, None]),
            "W_gcn": bf(np.random.standard_normal((C, C)) / np.sqrt(C) / s[:, None]),
            "b_gcn": bf(np.random.standard_normal(C) * 0.3)}


def reference(vma, vmr, W_gcn, b_gcn):
    vq = mxq(f64(vma), 0, "e4m3")
    A = vq.T @ vq
    e = np.exp(A - A.max(1, keepdims=True))
    x = (mxq(f64(vmr), 0, "e4m3").T @ mxq(f64(W_gcn), 0, "e4m3")) + f64(b_gcn)
    out = (mxq(e, 1, "e4m3") @ mxq(x, 0, "e4m3")) / e.sum(1, keepdims=True)
    return out.T

@@ -1,0 +1,276 @@
+from contextlib import ExitStack
+
+import concourse.mybir as mybir
+from concourse.masks import make_identity
+
+FP8X4 = mybir.dt.float8_e4m3fn_x4
+BF16 = mybir.dt.bfloat16
+F32 = mybir.dt.float32
+U32 = mybir.dt.uint32
+U8 = mybir.dt.uint8
+ALU = mybir.AluOpType
+ACT = mybir.ActivationFunctionType
+AXIS = mybir.AxisListType
+
+P = 128
+PACK = 4
+K_PASS = P * PACK
+SIZE = 1024
+PASSES = SIZE // K_PASS
+BLOCKS = SIZE // P
+BANK = 512
+HALVES = SIZE // BANK
+RUN = 4
+ROUND_BLOCKS = 2
+ROUND = ROUND_BLOCKS * P
+ROUNDS = SIZE // ROUND
+BLOCKS_PER_BANK = BANK // ROUND
+ROUND_BANKS = BLOCKS // BLOCKS_PER_BANK
+OUT_BANKS = ROUNDS * ROUND_BANKS
+X_BANKS = PASSES * BLOCKS
+FILL = 2
+X_STEPS = X_BANKS // 2 // FILL
+
+FLOPS = 3 * 2 * SIZE * SIZE * SIZE
+
+
+def tile_agcn_pb_kernel(tc, vma, vmr, W_gcn, b_gcn, out):
+    nc = tc.nc
+    with ExitStack() as stack:
+        keep = stack.enter_context(tc.tile_pool(name="keep", bufs=1))
+        stage = stack.enter_context(tc.tile_pool(name="stage", bufs=4))
+        small = stack.enter_context(tc.tile_pool(name="small", bufs=4))
+        psum = stack.enter_context(tc.psum_pool(name="psum", bufs=6))
+        psum_t = stack.enter_context(tc.psum_pool(name="psum_t", bufs=2))
+        stack.enter_context(tc.manual_schedule())
+
+        sources = {"vmr": vmr, "w": W_gcn, "vma": vma}
+        codes = {}
+        scales = {}
+        for name in ("vmr", "w", "vma", "x", "e"):
+            codes[name] = keep.tile([P, PASSES, SIZE], U32, name="codes_" + name, align_bytes=64)
+            scales[name] = keep.tile([P, PASSES, SIZE], U8, name="scales_" + name, align_bytes=64)
+
+
+        raw = {}
+        grouped = {}
+
+        def load(name, c, n):
+            raw[name, c, n] = keep.tile([P, PACK, BANK], BF16, name="raw_%s%d%d" % (name, c, n))
+            piece = sources[name][c * K_PASS : (c + 1) * K_PASS, n * BANK : (n + 1) * BANK]
+            nc.sync.dma_start(out=raw[name, c, n][:], in_=piece.rearrange("(p j) w -> p j w", j=PACK))
+
+        def regroup(copy, name, c, n):
+            grouped[name, c, n] = stage.tile([P, BANK, PACK], BF16, tag="grouped", name="grouped", align_bytes=64)
+            copy(
+                out=grouped[name, c, n][:].rearrange("p (w i) j -> p w j i", i=RUN),
+                in_=raw[name, c, n][:].rearrange("p j (w i) -> p w j i", i=RUN),
+            )
+
+        def quantise(name, c, first, values):
+            width = values.shape[1]
+            nc.vector.quantize_mx(
+                out=codes[name][:, c, first : first + width].bitcast(FP8X4),
+                scales=scales[name][:, c, first : first + width],
+                in_=values.rearrange("p w j -> p (w j)"),
+            )
+
+        def mx_group(acc, left, left_cols, right, right_cols):
+            for c in range(PASSES):
+                nc.tensor.matmul_mx(
+                    out=acc,
+                    lhsT=codes[left][:, c, left_cols].bitcast(FP8X4),
+                    lhsT_scale=scales[left][:, c, left_cols],
+                    rhs=codes[right][:, c, right_cols].bitcast(FP8X4),
+                    rhs_scale=scales[right][:, c, right_cols],
+                    start=(c == 0),
+                    stop=(c == PASSES - 1),
+                )
+
+        x_grouped = {}
+
+        def x_bank(k):
+            g, b = divmod(k, BLOCKS)
+            n, s = divmod(b, BANK // P)
+            channels = slice(b * P, (b + 1) * P)
+            x_acc = psum.tile([P, PACK, P], F32, tag="bank")
+            for t in range(PACK):
+                mx_group(x_acc[:, t, :], "vmr", slice((g * PACK + t) * P, (g * PACK + t + 1) * P), "w", channels)
+            if s == 0:
+                x_grouped[g, n] = stage.tile([P, BANK, PACK], BF16, tag="grouped", name="x_grouped", align_bytes=64)
+            nc.vector.tensor_tensor(
+                out=x_grouped[g, n][:, s * P : (s + 1) * P, :],
+                in0=x_acc[:].rearrange("p t w -> p w t"),
+                in1=bias_all[:, channels].unsqueeze(2).to_broadcast([P, P, PACK]),
+                op=ALU.add,
+            )
+            if s == BANK // P - 1:
+                quantise("x", g, n * BANK, x_grouped[g, n][:])
+
+        a_acc = {}
+        neg_max = {}
+        e_rows = {}
+        e_t = {}
+        e_grouped = {}
+
+        def a_rows(i):
+            for n in range(HALVES):
+                a_acc[i, n] = psum.tile([P, BANK], F32, tag="bank", name="a_acc")
+                mx_group(a_acc[i, n][:], "vma", slice(i * P, (i + 1) * P), "vma", slice(n * BANK, (n + 1) * BANK))
+
+        def row_max(i):
+            bank_max = small.tile([P, HALVES], F32, tag="bank_max")
+            for n in range(HALVES):
+                nc.vector.tensor_reduce(out=bank_max[:, n : n + 1], in_=a_acc[i, n][:], axis=AXIS.X, op=ALU.max)
+            neg_max[i] = small.tile([P, 1], F32, tag="neg_max", name="neg_max")
+            nc.vector.tensor_scalar(
+                out=neg_max[i][:],
+                in0=bank_max[:, 0:1],
+                scalar1=bank_max[:, 1:2],
+                scalar2=-1.0,
+                op0=ALU.max,
+                op1=ALU.mult,
+            )
+
+        def exp_rows(i):
+            e_rows[i] = stage.tile([P, SIZE], BF16, tag="e_rows", name="e_rows")
+            for n in range(HALVES):
+                nc.scalar.activation(
+                    out=e_rows[i][:, n * BANK : (n + 1) * BANK],
+                    in_=a_acc[i, n][:],
+                    func=ACT.Exp,
+                    bias=neg_max[i][:],
+                    scale=1.0,
+                    accum_out=row_sums[:, i, n : n + 1],
+                )
+
+        def transpose_rows(i):
+            e_t[i] = psum_t.tile([P, BLOCKS, P], BF16, tag="e_t", name="e_t")
+            for j in range(BLOCKS):
+                nc.tensor.transpose(e_t[i][:, j, :], e_rows[i][:, j * P : (j + 1) * P], ident_bf16[:])
+
+        def copy_out_rows(i):
+            r, q = divmod(i, ROUND_BLOCKS)
+            if q == 0:
+                e_grouped[r] = stage.tile(
+                    [P, PASSES, ROUND, PACK], BF16, tag="e_grouped", name="e_grouped", align_bytes=64
+                )
+            nc.scalar.copy(
+                out=e_grouped[r][:, :, q * P : (q + 1) * P, :],
+                in_=e_t[i][:].rearrange("p (g t) k -> p g k t", g=PASSES),
+            )
+
+        recip = {}
+
+        def quantise_round(r):
+            for g in range(PASSES):
+                quantise("e", g, r * ROUND, e_grouped[r][:, g, :, :])
+            sums = small.tile([P, ROUND_BLOCKS], F32, tag="sums")
+            nc.vector.tensor_reduce(
+                out=sums[:], in_=row_sums[:, r * ROUND_BLOCKS : (r + 1) * ROUND_BLOCKS, :], axis=AXIS.X, op=ALU.add
+            )
+            recip[r] = small.tile([P, ROUND_BLOCKS], F32, tag="recip", name="recip")
+            nc.vector.reciprocal(out=recip[r][:], in_=sums[:])
+
+        def spread_recip(r):
+            positions = slice(r * ROUND, (r + 1) * ROUND)
+            recip_acc = psum.tile([P, ROUND_BLOCKS, P], F32, tag="bank")
+            for q in range(ROUND_BLOCKS):
+                nc.tensor.matmul(
+                    out=recip_acc[:, q, :],
+                    lhsT=recip[r][:, q : q + 1].to_broadcast([P, P]),
+                    rhs=ident_f32[:],
+                    start=True,
+                    stop=True,
+                )
+            nc.scalar.copy(out=recip_all[:, positions], in_=recip_acc[:].rearrange("p q k -> p (q k)"))
+
+        def out_bank(k):
+            r, pair = divmod(k, ROUND_BANKS)
+            positions = slice(r * ROUND, (r + 1) * ROUND)
+            first = pair * BLOCKS_PER_BANK * P
+            out_acc = psum.tile([P, BLOCKS_PER_BANK, ROUND], F32, tag="bank")
+            for s in range(BLOCKS_PER_BANK):
+                mx_group(out_acc[:, s, :], "x", slice(first + s * P, first + (s + 1) * P), "e", positions)
+            result = stage.tile([P, BLOCKS_PER_BANK, ROUND], F32, tag="result", bufs=8)
+            nc.vector.tensor_tensor(
+                out=result[:],
+                in0=out_acc[:],
+                in1=recip_all[:, positions].unsqueeze(1).to_broadcast([P, BLOCKS_PER_BANK, ROUND]),
+                op=ALU.mult,
+            )
+            nc.sync.dma_start(
+                out=out[first : first + BLOCKS_PER_BANK * P, positions].rearrange("(s p) k -> p s k", p=P),
+                in_=result[:],
+            )
+
+
+        bias_row = keep.tile([P, SIZE], BF16, name="bias_row")
+        nc.vector.memset(bias_row[:], 0.0)
+        nc.sync.dma_start(out=bias_row[0:1, :], in_=b_gcn.unsqueeze(0))
+        x_inputs = (("vmr", 0), ("w", 0), ("vmr", 1), ("w", 1))
+        for name, c in x_inputs + (("vma", 0), ("vma", 1)):
+            for n in range(HALVES):
+                load(name, c, n)
+
+        ident_bf16 = keep.tile([P, P], BF16, name="ident_bf16")
+        make_identity(nc, ident_bf16[:])
+        ident_f32 = keep.tile([P, P], F32, name="ident_f32")
+        make_identity(nc, ident_f32[:])
+        row_sums = keep.tile([P, BLOCKS, HALVES], F32, name="row_sums")
+        recip_all = keep.tile([P, SIZE], F32, name="recip_all")
+
+        ones = keep.tile([P, P], BF16, name="ones")
+        nc.vector.memset(ones[:], 1.0)
+        bias_all = keep.tile([P, SIZE], BF16, name="bias_all")
+        for n in range(HALVES):
+            bias_acc = psum.tile([P, BANK], F32, tag="bank")
+            nc.tensor.matmul(
+                out=bias_acc[:], lhsT=ones[:], rhs=bias_row[:, n * BANK : (n + 1) * BANK], start=True, stop=True
+            )
+            nc.scalar.copy(out=bias_all[:, n * BANK : (n + 1) * BANK], in_=bias_acc[:])
+
+        for k, (name, c) in enumerate(x_inputs):
+            regroup(nc.vector.tensor_copy, name, c, 0)
+            regroup(nc.scalar.copy, name, c, 1)
+            if k > 0:
+                quantise(x_inputs[k - 1][0], x_inputs[k - 1][1], BANK, grouped[x_inputs[k - 1] + (1,)][:])
+            quantise(name, c, 0, grouped[name, c, 0][:])
+        quantise(name, c, BANK, grouped[name, c, 1][:])
+
+        for k in range(PASSES * HALVES):
+            regroup(nc.scalar.copy, "vma", k // HALVES, k % HALVES)
+            x_bank(FILL * k)
+            x_bank(FILL * k + 1)
+            if k > 0:
+                quantise("vma", (k - 1) // HALVES, (k - 1) % HALVES * BANK, grouped["vma", (k - 1) // HALVES, (k - 1) % HALVES][:])
+        quantise("vma", PASSES - 1, BANK, grouped["vma", PASSES - 1, HALVES - 1][:])
+
+        a_rows(0)
+        row_max(0)
+        for i in range(BLOCKS + 1):
+            if i > 0:
+                transpose_rows(i - 1)
+            if i < BLOCKS:
+                exp_rows(i)
+            if i + 1 < BLOCKS:
+                a_rows(i + 1)
+            if i > 0:
+                copy_out_rows(i - 1)
+            if i + 1 < BLOCKS:
+                row_max(i + 1)
+            if i < X_STEPS:
+                x_bank(X_BANKS // 2 + FILL * i)
+                x_bank(X_BANKS // 2 + FILL * i + 1)
+            else:
+                out_bank(FILL * (i - X_STEPS))
+                out_bank(FILL * (i - X_STEPS) + 1)
+            if i > 0 and i % ROUND_BLOCKS == 0:
+                quantise_round(i // ROUND_BLOCKS - 1)
+            if i >= 3 and i % ROUND_BLOCKS == 1:
+                spread_recip((i - 3) // ROUND_BLOCKS)
+        for k in range(FILL * (BLOCKS + 1 - X_STEPS), OUT_BANKS - ROUND_BANKS):
+            out_bank(k)
+        spread_recip(ROUNDS - 1)
+        for k in range(OUT_BANKS - ROUND_BANKS, OUT_BANKS):
+            out_bank(k)

@@ -42,7 +42,6 @@ def tile_agcn_pb_kernel(tc, vma, vmr, W_gcn, b_gcn, out):
         small = stack.enter_context(tc.tile_pool(name="small", bufs=4))
         psum = stack.enter_context(tc.psum_pool(name="psum", bufs=6))
         psum_t = stack.enter_context(tc.psum_pool(name="psum_t", bufs=2))
-        stack.enter_context(tc.manual_schedule())
 
         sources = {"vmr": vmr, "w": W_gcn, "vma": vma}
         codes = {}

@@ -54,16 +54,16 @@ def tile_agcn_pb_kernel(tc, vma, vmr, W_gcn, b_gcn, out):
         raw = {}
         grouped = {}
 
-        def load(name, c, n):
-            raw[name, c, n] = keep.tile([P, PACK, BANK], BF16, name="raw_%s%d%d" % (name, c, n))
-            piece = sources[name][c * K_PASS : (c + 1) * K_PASS, n * BANK : (n + 1) * BANK]
-            nc.sync.dma_start(out=raw[name, c, n][:], in_=piece.rearrange("(p j) w -> p j w", j=PACK))
+        def load(name, c):
+            raw[name, c] = keep.tile([P, PACK, SIZE], BF16, name="raw_%s%d" % (name, c))
+            rows = sources[name][c * K_PASS : (c + 1) * K_PASS, :]
+            nc.sync.dma_start(out=raw[name, c][:], in_=rows.rearrange("(p j) w -> p j w", j=PACK))
 
         def regroup(copy, name, c, n):
             grouped[name, c, n] = stage.tile([P, BANK, PACK], BF16, tag="grouped", name="grouped", align_bytes=64)
             copy(
                 out=grouped[name, c, n][:].rearrange("p (w i) j -> p w j i", i=RUN),
-                in_=raw[name, c, n][:].rearrange("p j (w i) -> p w j i", i=RUN),
+                in_=raw[name, c][:, :, n * BANK : (n + 1) * BANK].rearrange("p j (w i) -> p w j i", i=RUN),
             )
 
         def quantise(name, c, first, values):
@@ -209,8 +209,7 @@ def tile_agcn_pb_kernel(tc, vma, vmr, W_gcn, b_gcn, out):
         nc.sync.dma_start(out=bias_row[0:1, :], in_=b_gcn.unsqueeze(0))
         x_inputs = (("vmr", 0), ("w", 0), ("vmr", 1), ("w", 1))
         for name, c in x_inputs + (("vma", 0), ("vma", 1)):
-            for n in range(HALVES):
-                load(name, c, n)
+            load(name, c)
 
         ident_bf16 = keep.tile([P, P], BF16, name="ident_bf16")
         make_identity(nc, ident_bf16[:])

@@ -21,6 +21,7 @@ BLOCKS = SIZE // P
 BANK = 512
 HALVES = SIZE // BANK
 RUN = 4
+
 ROUND_BLOCKS = 2
 ROUND = ROUND_BLOCKS * P
 ROUNDS = SIZE // ROUND
@@ -28,8 +29,14 @@ BLOCKS_PER_BANK = BANK // ROUND
 ROUND_BANKS = BLOCKS // BLOCKS_PER_BANK
 OUT_BANKS = ROUNDS * ROUND_BANKS
 X_BANKS = PASSES * BLOCKS
+
+TRANSPOSE_BANKS = 2
+WORK_BANKS = 6
+LEAD = WORK_BANKS - HALVES
 FILL = 2
-X_STEPS = X_BANKS // 2 // FILL
+EARLY = LEAD + FILL
+STAGE_BUFS = 4
+RESULT_BUFS = 8
 
 FLOPS = 3 * 2 * SIZE * SIZE * SIZE
 
@@ -38,10 +45,10 @@ def tile_agcn_pb_kernel(tc, vma, vmr, W_gcn, b_gcn, out):
     nc = tc.nc
     with ExitStack() as stack:
         keep = stack.enter_context(tc.tile_pool(name="keep", bufs=1))
-        stage = stack.enter_context(tc.tile_pool(name="stage", bufs=4))
-        small = stack.enter_context(tc.tile_pool(name="small", bufs=4))
-        psum = stack.enter_context(tc.psum_pool(name="psum", bufs=6))
-        psum_t = stack.enter_context(tc.psum_pool(name="psum_t", bufs=2))
+        stage = stack.enter_context(tc.tile_pool(name="stage", bufs=STAGE_BUFS))
+        small = stack.enter_context(tc.tile_pool(name="small", bufs=STAGE_BUFS))
+        psum = stack.enter_context(tc.psum_pool(name="psum", bufs=WORK_BANKS))
+        psum_t = stack.enter_context(tc.psum_pool(name="psum_t", bufs=TRANSPOSE_BANKS))
 
         sources = {"vmr": vmr, "w": W_gcn, "vma": vma}
         codes = {}
@@ -74,6 +81,9 @@ def tile_agcn_pb_kernel(tc, vma, vmr, W_gcn, b_gcn, out):
                 in_=values.rearrange("p w j -> p (w j)"),
             )
 
+        def quantise_piece(name, c, n):
+            quantise(name, c, n * BANK, grouped[name, c, n][:])
+
         def mx_group(acc, left, left_cols, right, right_cols):
             for c in range(PASSES):
                 nc.tensor.matmul_mx(
@@ -86,20 +96,27 @@ def tile_agcn_pb_kernel(tc, vma, vmr, W_gcn, b_gcn, out):
                     stop=(c == PASSES - 1),
                 )
 
+        x_acc = {}
         x_grouped = {}
 
+        def x_matmuls(k):
+            g, b = divmod(k, BLOCKS)
+            x_acc[k] = psum.tile([P, PACK, P], F32, tag="bank", name="x_acc")
+            for t in range(PACK):
+                nodes = slice((g * PACK + t) * P, (g * PACK + t + 1) * P)
+                mx_group(x_acc[k][:, t, :], "vmr", nodes, "w", slice(b * P, (b + 1) * P))
+
         def x_bank(k):
+            if k + LEAD < X_BANKS:
+                x_matmuls(k + LEAD)
             g, b = divmod(k, BLOCKS)
             n, s = divmod(b, BANK // P)
             channels = slice(b * P, (b + 1) * P)
-            x_acc = psum.tile([P, PACK, P], F32, tag="bank")
-            for t in range(PACK):
-                mx_group(x_acc[:, t, :], "vmr", slice((g * PACK + t) * P, (g * PACK + t + 1) * P), "w", channels)
             if s == 0:
                 x_grouped[g, n] = stage.tile([P, BANK, PACK], BF16, tag="grouped", name="x_grouped", align_bytes=64)
             nc.vector.tensor_tensor(
                 out=x_grouped[g, n][:, s * P : (s + 1) * P, :],
-                in0=x_acc[:].rearrange("p t w -> p w t"),
+                in0=x_acc[k][:].rearrange("p t w -> p w t"),
                 in1=bias_all[:, channels].unsqueeze(2).to_broadcast([P, P, PACK]),
                 op=ALU.add,
             )
@@ -111,6 +128,7 @@ def tile_agcn_pb_kernel(tc, vma, vmr, W_gcn, b_gcn, out):
         e_rows = {}
         e_t = {}
         e_grouped = {}
+        recip = {}
 
         def a_rows(i):
             for n in range(HALVES):
@@ -159,8 +177,6 @@ def tile_agcn_pb_kernel(tc, vma, vmr, W_gcn, b_gcn, out):
                 in_=e_t[i][:].rearrange("p (g t) k -> p g k t", g=PASSES),
             )
 
-        recip = {}
-
         def quantise_round(r):
             for g in range(PASSES):
                 quantise("e", g, r * ROUND, e_grouped[r][:, g, :, :])
@@ -175,13 +191,16 @@ def tile_agcn_pb_kernel(tc, vma, vmr, W_gcn, b_gcn, out):
             positions = slice(r * ROUND, (r + 1) * ROUND)
             recip_acc = psum.tile([P, ROUND_BLOCKS, P], F32, tag="bank")
             for q in range(ROUND_BLOCKS):
-                nc.tensor.matmul(
-                    out=recip_acc[:, q, :],
-                    lhsT=recip[r][:, q : q + 1].to_broadcast([P, P]),
-                    rhs=ident_f32[:],
-                    start=True,
-                    stop=True,
+                repeated = small.tile([P, P], F32, tag="repeated")
+                nc.gpsimd.tensor_scalar(
+                    out=repeated[:],
+                    in0=ones_f32[:],
+                    scalar1=recip[r][:, q : q + 1],
+                    scalar2=0.0,
+                    op0=ALU.mult,
+                    op1=ALU.add,
                 )
+                nc.tensor.transpose(recip_acc[:, q, :], repeated[:], ident_f32[:])
             nc.scalar.copy(out=recip_all[:, positions], in_=recip_acc[:].rearrange("p q k -> p (q k)"))
 
         def out_bank(k):
@@ -191,7 +210,7 @@ def tile_agcn_pb_kernel(tc, vma, vmr, W_gcn, b_gcn, out):
             out_acc = psum.tile([P, BLOCKS_PER_BANK, ROUND], F32, tag="bank")
             for s in range(BLOCKS_PER_BANK):
                 mx_group(out_acc[:, s, :], "x", slice(first + s * P, first + (s + 1) * P), "e", positions)
-            result = stage.tile([P, BLOCKS_PER_BANK, ROUND], F32, tag="result", bufs=8)
+            result = stage.tile([P, BLOCKS_PER_BANK, ROUND], F32, tag="result", bufs=RESULT_BUFS)
             nc.vector.tensor_tensor(
                 out=result[:],
                 in0=out_acc[:],
@@ -202,6 +221,12 @@ def tile_agcn_pb_kernel(tc, vma, vmr, W_gcn, b_gcn, out):
                 out=out[first : first + BLOCKS_PER_BANK * P, positions].rearrange("(s p) k -> p s k", p=P),
                 in_=result[:],
             )
+
+        def side_bank(k):
+            if k < X_BANKS:
+                x_bank(k)
+            else:
+                out_bank(k - X_BANKS)
 
 
         bias_row = keep.tile([P, SIZE], BF16, name="bias_row")
@@ -215,6 +240,8 @@ def tile_agcn_pb_kernel(tc, vma, vmr, W_gcn, b_gcn, out):
         make_identity(nc, ident_bf16[:])
         ident_f32 = keep.tile([P, P], F32, name="ident_f32")
         make_identity(nc, ident_f32[:])
+        ones_f32 = keep.tile([P, P], F32, name="ones_f32")
+        nc.gpsimd.memset(ones_f32[:], 1.0)
         row_sums = keep.tile([P, BLOCKS, HALVES], F32, name="row_sums")
         recip_all = keep.tile([P, SIZE], F32, name="recip_all")
 
@@ -228,47 +255,56 @@ def tile_agcn_pb_kernel(tc, vma, vmr, W_gcn, b_gcn, out):
             )
             nc.scalar.copy(out=bias_all[:, n * BANK : (n + 1) * BANK], in_=bias_acc[:])
 
-        for k, (name, c) in enumerate(x_inputs):
+        previous = None
+        for name, c in x_inputs:
             regroup(nc.vector.tensor_copy, name, c, 0)
             regroup(nc.scalar.copy, name, c, 1)
-            if k > 0:
-                quantise(x_inputs[k - 1][0], x_inputs[k - 1][1], BANK, grouped[x_inputs[k - 1] + (1,)][:])
-            quantise(name, c, 0, grouped[name, c, 0][:])
-        quantise(name, c, BANK, grouped[name, c, 1][:])
+            if previous is not None:
+                quantise_piece(previous[0], previous[1], 1)
+            quantise_piece(name, c, 0)
+            previous = (name, c)
+        quantise_piece(previous[0], previous[1], 1)
 
-        for k in range(PASSES * HALVES):
-            regroup(nc.scalar.copy, "vma", k // HALVES, k % HALVES)
-            x_bank(FILL * k)
-            x_bank(FILL * k + 1)
-            if k > 0:
-                quantise("vma", (k - 1) // HALVES, (k - 1) % HALVES * BANK, grouped["vma", (k - 1) // HALVES, (k - 1) % HALVES][:])
-        quantise("vma", PASSES - 1, BANK, grouped["vma", PASSES - 1, HALVES - 1][:])
+        for k in range(LEAD):
+            x_matmuls(k)
+        regroup(nc.scalar.copy, "vma", 0, 0)
+        regroup(nc.vector.tensor_copy, "vma", 0, 1)
+        side_bank(0)
+        side_bank(1)
+        regroup(nc.scalar.copy, "vma", 1, 0)
+        quantise_piece("vma", 0, 1)
+        quantise_piece("vma", 0, 0)
+        side_bank(2)
+        side_bank(3)
+        regroup(nc.scalar.copy, "vma", 1, 1)
+        quantise_piece("vma", 1, 0)
+        quantise_piece("vma", 1, 1)
 
         a_rows(0)
+        for k in range(LEAD, EARLY):
+            side_bank(k)
         row_max(0)
         for i in range(BLOCKS + 1):
-            if i > 0:
+            if i >= 1:
                 transpose_rows(i - 1)
             if i < BLOCKS:
                 exp_rows(i)
             if i + 1 < BLOCKS:
                 a_rows(i + 1)
-            if i > 0:
+            if i >= 1:
                 copy_out_rows(i - 1)
             if i + 1 < BLOCKS:
                 row_max(i + 1)
-            if i < X_STEPS:
-                x_bank(X_BANKS // 2 + FILL * i)
-                x_bank(X_BANKS // 2 + FILL * i + 1)
-            else:
-                out_bank(FILL * (i - X_STEPS))
-                out_bank(FILL * (i - X_STEPS) + 1)
-            if i > 0 and i % ROUND_BLOCKS == 0:
-                quantise_round(i // ROUND_BLOCKS - 1)
-            if i >= 3 and i % ROUND_BLOCKS == 1:
-                spread_recip((i - 3) // ROUND_BLOCKS)
-        for k in range(FILL * (BLOCKS + 1 - X_STEPS), OUT_BANKS - ROUND_BANKS):
-            out_bank(k)
+            for k in range(EARLY + FILL * i, EARLY + FILL * (i + 1)):
+                side_bank(k)
+            if i >= 1 and (i - 1) % ROUND_BLOCKS == ROUND_BLOCKS - 1:
+                quantise_round((i - 1) // ROUND_BLOCKS)
+            if i >= 2 and (i - 2) % ROUND_BLOCKS == ROUND_BLOCKS - 1:
+                spread_recip((i - 2) // ROUND_BLOCKS)
+
+        last_round = X_BANKS + OUT_BANKS - ROUND_BANKS
+        for k in range(EARLY + FILL * (BLOCKS + 1), last_round):
+            side_bank(k)
         spread_recip(ROUNDS - 1)
-        for k in range(OUT_BANKS - ROUND_BANKS, OUT_BANKS):
-            out_bank(k)
+        for k in range(last_round, X_BANKS + OUT_BANKS):
+            side_bank(k)

from contextlib import ExitStack

import concourse.mybir as mybir
from concourse.masks import make_identity

FP8X4 = mybir.dt.float8_e4m3fn_x4
BF16 = mybir.dt.bfloat16
F32 = mybir.dt.float32
U32 = mybir.dt.uint32
U8 = mybir.dt.uint8
ALU = mybir.AluOpType
ACT = mybir.ActivationFunctionType
AXIS = mybir.AxisListType

P = 128
PACK = 4
K_PASS = P * PACK
SIZE = 1024
PASSES = SIZE // K_PASS
BLOCKS = SIZE // P
BANK = 512
HALVES = SIZE // BANK
RUN = 4

ROUND_BLOCKS = 2
ROUND = ROUND_BLOCKS * P
ROUNDS = SIZE // ROUND
BLOCKS_PER_BANK = BANK // ROUND
ROUND_BANKS = BLOCKS // BLOCKS_PER_BANK
OUT_BANKS = ROUNDS * ROUND_BANKS
X_BANKS = PASSES * BLOCKS

TRANSPOSE_BANKS = 2
WORK_BANKS = 6
LEAD = WORK_BANKS - HALVES
FILL = 2
EARLY = LEAD + FILL
STAGE_BUFS = 4
RESULT_BUFS = 8

FLOPS = 3 * 2 * SIZE * SIZE * SIZE


def tile_agcn_pb_kernel(tc, vma, vmr, W_gcn, b_gcn, out):
    nc = tc.nc
    with ExitStack() as stack:
        keep = stack.enter_context(tc.tile_pool(name="keep", bufs=1))
        stage = stack.enter_context(tc.tile_pool(name="stage", bufs=STAGE_BUFS))
        small = stack.enter_context(tc.tile_pool(name="small", bufs=STAGE_BUFS))
        psum = stack.enter_context(tc.psum_pool(name="psum", bufs=WORK_BANKS))
        psum_t = stack.enter_context(tc.psum_pool(name="psum_t", bufs=TRANSPOSE_BANKS))

        sources = {"vmr": vmr, "w": W_gcn, "vma": vma}
        codes = {}
        scales = {}
        for name in ("vmr", "w", "vma", "x", "e"):
            codes[name] = keep.tile([P, PASSES, SIZE], U32, name="codes_" + name, align_bytes=64)
            scales[name] = keep.tile([P, PASSES, SIZE], U8, name="scales_" + name, align_bytes=64)


        raw = {}
        grouped = {}

        def load(name, c):
            raw[name, c] = keep.tile([P, PACK, SIZE], BF16, name="raw_%s%d" % (name, c))
            rows = sources[name][c * K_PASS : (c + 1) * K_PASS, :]
            nc.sync.dma_start(out=raw[name, c][:], in_=rows.rearrange("(p j) w -> p j w", j=PACK))

        def regroup(copy, name, c, n):
            grouped[name, c, n] = stage.tile([P, BANK, PACK], BF16, tag="grouped", name="grouped", align_bytes=64)
            copy(
                out=grouped[name, c, n][:].rearrange("p (w i) j -> p w j i", i=RUN),
                in_=raw[name, c][:, :, n * BANK : (n + 1) * BANK].rearrange("p j (w i) -> p w j i", i=RUN),
            )

        def quantise(name, c, first, values):
            width = values.shape[1]
            nc.vector.quantize_mx(
                out=codes[name][:, c, first : first + width].bitcast(FP8X4),
                scales=scales[name][:, c, first : first + width],
                in_=values.rearrange("p w j -> p (w j)"),
            )

        def quantise_piece(name, c, n):
            quantise(name, c, n * BANK, grouped[name, c, n][:])

        def mx_group(acc, left, left_cols, right, right_cols):
            for c in range(PASSES):
                nc.tensor.matmul_mx(
                    out=acc,
                    lhsT=codes[left][:, c, left_cols].bitcast(FP8X4),
                    lhsT_scale=scales[left][:, c, left_cols],
                    rhs=codes[right][:, c, right_cols].bitcast(FP8X4),
                    rhs_scale=scales[right][:, c, right_cols],
                    start=(c == 0),
                    stop=(c == PASSES - 1),
                )

        x_acc = {}
        x_grouped = {}

        def x_matmuls(k):
            g, b = divmod(k, BLOCKS)
            x_acc[k] = psum.tile([P, PACK, P], F32, tag="bank", name="x_acc")
            for t in range(PACK):
                nodes = slice((g * PACK + t) * P, (g * PACK + t + 1) * P)
                mx_group(x_acc[k][:, t, :], "vmr", nodes, "w", slice(b * P, (b + 1) * P))

        def x_bank(k):
            if k + LEAD < X_BANKS:
                x_matmuls(k + LEAD)
            g, b = divmod(k, BLOCKS)
            n, s = divmod(b, BANK // P)
            channels = slice(b * P, (b + 1) * P)
            if s == 0:
                x_grouped[g, n] = stage.tile([P, BANK, PACK], BF16, tag="grouped", name="x_grouped", align_bytes=64)
            nc.vector.tensor_tensor(
                out=x_grouped[g, n][:, s * P : (s + 1) * P, :],
                in0=x_acc[k][:].rearrange("p t w -> p w t"),
                in1=bias_all[:, channels].unsqueeze(2).to_broadcast([P, P, PACK]),
                op=ALU.add,
            )
            if s == BANK // P - 1:
                quantise("x", g, n * BANK, x_grouped[g, n][:])

        a_acc = {}
        neg_max = {}
        e_rows = {}
        e_t = {}
        e_grouped = {}
        recip = {}

        def a_rows(i):
            for n in range(HALVES):
                a_acc[i, n] = psum.tile([P, BANK], F32, tag="bank", name="a_acc")
                mx_group(a_acc[i, n][:], "vma", slice(i * P, (i + 1) * P), "vma", slice(n * BANK, (n + 1) * BANK))

        def row_max(i):
            bank_max = small.tile([P, HALVES], F32, tag="bank_max")
            for n in range(HALVES):
                nc.vector.tensor_reduce(out=bank_max[:, n : n + 1], in_=a_acc[i, n][:], axis=AXIS.X, op=ALU.max)
            neg_max[i] = small.tile([P, 1], F32, tag="neg_max", name="neg_max")
            nc.vector.tensor_scalar(
                out=neg_max[i][:],
                in0=bank_max[:, 0:1],
                scalar1=bank_max[:, 1:2],
                scalar2=-1.0,
                op0=ALU.max,
                op1=ALU.mult,
            )

        def exp_rows(i):
            e_rows[i] = stage.tile([P, SIZE], BF16, tag="e_rows", name="e_rows")
            for n in range(HALVES):
                nc.scalar.activation(
                    out=e_rows[i][:, n * BANK : (n + 1) * BANK],
                    in_=a_acc[i, n][:],
                    func=ACT.Exp,
                    bias=neg_max[i][:],
                    scale=1.0,
                    accum_out=row_sums[:, i, n : n + 1],
                )

        def transpose_rows(i):
            e_t[i] = psum_t.tile([P, BLOCKS, P], BF16, tag="e_t", name="e_t")
            for j in range(BLOCKS):
                nc.tensor.transpose(e_t[i][:, j, :], e_rows[i][:, j * P : (j + 1) * P], ident_bf16[:])

        def copy_out_rows(i):
            r, q = divmod(i, ROUND_BLOCKS)
            if q == 0:
                e_grouped[r] = stage.tile(
                    [P, PASSES, ROUND, PACK], BF16, tag="e_grouped", name="e_grouped", align_bytes=64
                )
            nc.scalar.copy(
                out=e_grouped[r][:, :, q * P : (q + 1) * P, :],
                in_=e_t[i][:].rearrange("p (g t) k -> p g k t", g=PASSES),
            )

        def quantise_round(r):
            for g in range(PASSES):
                quantise("e", g, r * ROUND, e_grouped[r][:, g, :, :])
            sums = small.tile([P, ROUND_BLOCKS], F32, tag="sums")
            nc.vector.tensor_reduce(
                out=sums[:], in_=row_sums[:, r * ROUND_BLOCKS : (r + 1) * ROUND_BLOCKS, :], axis=AXIS.X, op=ALU.add
            )
            recip[r] = small.tile([P, ROUND_BLOCKS], F32, tag="recip", name="recip")
            nc.vector.reciprocal(out=recip[r][:], in_=sums[:])

        def spread_recip(r):
            positions = slice(r * ROUND, (r + 1) * ROUND)
            recip_acc = psum.tile([P, ROUND_BLOCKS, P], F32, tag="bank")
            for q in range(ROUND_BLOCKS):
                repeated = small.tile([P, P], F32, tag="repeated")
                nc.gpsimd.tensor_scalar(
                    out=repeated[:],
                    in0=ones_f32[:],
                    scalar1=recip[r][:, q : q + 1],
                    scalar2=0.0,
                    op0=ALU.mult,
                    op1=ALU.add,
                )
                nc.tensor.transpose(recip_acc[:, q, :], repeated[:], ident_f32[:])
            nc.scalar.copy(out=recip_all[:, positions], in_=recip_acc[:].rearrange("p q k -> p (q k)"))

        def out_bank(k):
            r, pair = divmod(k, ROUND_BANKS)
            positions = slice(r * ROUND, (r + 1) * ROUND)
            first = pair * BLOCKS_PER_BANK * P
            out_acc = psum.tile([P, BLOCKS_PER_BANK, ROUND], F32, tag="bank")
            for s in range(BLOCKS_PER_BANK):
                mx_group(out_acc[:, s, :], "x", slice(first + s * P, first + (s + 1) * P), "e", positions)
            result = stage.tile([P, BLOCKS_PER_BANK, ROUND], F32, tag="result", bufs=RESULT_BUFS)
            nc.vector.tensor_tensor(
                out=result[:],
                in0=out_acc[:],
                in1=recip_all[:, positions].unsqueeze(1).to_broadcast([P, BLOCKS_PER_BANK, ROUND]),
                op=ALU.mult,
            )
            nc.sync.dma_start(
                out=out[first : first + BLOCKS_PER_BANK * P, positions].rearrange("(s p) k -> p s k", p=P),
                in_=result[:],
            )

        def side_bank(k):
            if k < X_BANKS:
                x_bank(k)
            else:
                out_bank(k - X_BANKS)


        bias_row = keep.tile([P, SIZE], BF16, name="bias_row")
        nc.vector.memset(bias_row[:], 0.0)
        nc.sync.dma_start(out=bias_row[0:1, :], in_=b_gcn.unsqueeze(0))
        x_inputs = (("vmr", 0), ("w", 0), ("vmr", 1), ("w", 1))
        for name, c in x_inputs + (("vma", 0), ("vma", 1)):
            load(name, c)

        ident_bf16 = keep.tile([P, P], BF16, name="ident_bf16")
        make_identity(nc, ident_bf16[:])
        ident_f32 = keep.tile([P, P], F32, name="ident_f32")
        make_identity(nc, ident_f32[:])
        ones_f32 = keep.tile([P, P], F32, name="ones_f32")
        nc.gpsimd.memset(ones_f32[:], 1.0)
        row_sums = keep.tile([P, BLOCKS, HALVES], F32, name="row_sums")
        recip_all = keep.tile([P, SIZE], F32, name="recip_all")

        ones = keep.tile([P, P], BF16, name="ones")
        nc.vector.memset(ones[:], 1.0)
        bias_all = keep.tile([P, SIZE], BF16, name="bias_all")
        for n in range(HALVES):
            bias_acc = psum.tile([P, BANK], F32, tag="bank")
            nc.tensor.matmul(
                out=bias_acc[:], lhsT=ones[:], rhs=bias_row[:, n * BANK : (n + 1) * BANK], start=True, stop=True
            )
            nc.scalar.copy(out=bias_all[:, n * BANK : (n + 1) * BANK], in_=bias_acc[:])

        previous = None
        for name, c in x_inputs:
            regroup(nc.vector.tensor_copy, name, c, 0)
            regroup(nc.scalar.copy, name, c, 1)
            if previous is not None:
                quantise_piece(previous[0], previous[1], 1)
            quantise_piece(name, c, 0)
            previous = (name, c)
        quantise_piece(previous[0], previous[1], 1)

        for k in range(LEAD):
            x_matmuls(k)
        regroup(nc.scalar.copy, "vma", 0, 0)
        regroup(nc.vector.tensor_copy, "vma", 0, 1)
        side_bank(0)
        side_bank(1)
        regroup(nc.scalar.copy, "vma", 1, 0)
        quantise_piece("vma", 0, 1)
        quantise_piece("vma", 0, 0)
        side_bank(2)
        side_bank(3)
        regroup(nc.scalar.copy, "vma", 1, 1)
        quantise_piece("vma", 1, 0)
        quantise_piece("vma", 1, 1)

        a_rows(0)
        for k in range(LEAD, EARLY):
            side_bank(k)
        row_max(0)
        for i in range(BLOCKS + 1):
            if i >= 1:
                transpose_rows(i - 1)
            if i < BLOCKS:
                exp_rows(i)
            if i + 1 < BLOCKS:
                a_rows(i + 1)
            if i >= 1:
                copy_out_rows(i - 1)
            if i + 1 < BLOCKS:
                row_max(i + 1)
            for k in range(EARLY + FILL * i, EARLY + FILL * (i + 1)):
                side_bank(k)
            if i >= 1 and (i - 1) % ROUND_BLOCKS == ROUND_BLOCKS - 1:
                quantise_round((i - 1) // ROUND_BLOCKS)
            if i >= 2 and (i - 2) % ROUND_BLOCKS == ROUND_BLOCKS - 1:
                spread_recip((i - 2) // ROUND_BLOCKS)

        last_round = X_BANKS + OUT_BANKS - ROUND_BANKS
        for k in range(EARLY + FILL * (BLOCKS + 1), last_round):
            side_bank(k)
        spread_recip(ROUNDS - 1)
        for k in range(last_round, X_BANKS + OUT_BANKS):
            side_bank(k)
